import numpy as np
import ml_dtypes


def mxq(x, axis, fmt="e4m3"):
    dtype, down = {"e4m3": (ml_dtypes.float8_e4m3fn, 7), "e5m2": (ml_dtypes.float8_e5m2, 14)}[fmt]
    v = np.moveaxis(np.asarray(x, np.float32).astype(ml_dtypes.bfloat16).astype(np.float64), axis, -1)
    blocks = v.reshape(v.shape[:-1] + (-1, 32))
    amax = np.abs(blocks).max(-1, keepdims=True)
    byte = np.maximum(np.where(amax > 0, np.frexp(amax)[1] - 1 + 127, 0) - down, 1)
    scale = np.exp2(byte - 127.0)
    codes = (blocks / scale).astype(np.float32).astype(dtype).astype(np.float64)
    return np.moveaxis((codes * scale).reshape(v.shape), -1, axis)


WIDE = False


def mx_kscale(k):
    if not WIDE:
        return np.ones(k)
    levels = np.array([10, -10, 5, -5, 0])
    a = np.random.permutation(np.resize(levels, k // 512 * 4)).reshape(k // 512, 4)
    idx = np.arange(k)
    return np.exp2(a[idx // 512, idx % 128 // 32])


BF16 = ml_dtypes.bfloat16


def bf(x):
    return np.asarray(x, np.float32).astype(BF16)


def f64(x):
    return np.asarray(x).astype(np.float64)


E2M1 = np.array([0.0, 0.5, 1.0, 1.5, 2.0, 3.0, 4.0, 6.0, -0.0, -0.5, -1.0, -1.5, -2.0, -3.0, -4.0, -6.0])


def pack_weight(w, fmt):
    k, n = w.shape
    w = f64(bf(w)).reshape(k // 32, 32, n)
    amax = np.abs(w).max(1)
    if fmt == "e4m3":
        byte = np.frexp(amax)[1] - 1 + 127 - 7
    else:
        mant, ex = np.frexp(amax / 6.0)
        byte = np.where(mant > 0.5, ex, ex - 1) + 127
    byte = np.clip(np.where(amax > 0, byte, 1), 1, 254)
    scaled = (w * np.exp2(127.0 - byte)[:, None, :]).reshape(k, n).astype(np.float32)
    by_word = np.ascontiguousarray(scaled.reshape(k // 512, 128, 4, n).transpose(0, 1, 3, 2))
    if fmt == "e4m3":
        words = by_word.astype(ml_dtypes.float8_e4m3fn).view(np.uint8)
    else:
        c = by_word.astype(ml_dtypes.float4_e2m1fn).view(np.uint8) & 0xF
        words = c[..., 0::2] | (c[..., 1::2] << 4)
    return np.ascontiguousarray(words), np.ascontiguousarray(byte.astype(np.uint8).reshape(k // 512, 16, n))


def unpack_weight(words, scales, fmt):
    g, p, n, _ = words.shape
    if fmt == "e4m3":
        vals = np.ascontiguousarray(words).view(ml_dtypes.float8_e4m3fn).astype(np.float64)
    else:
        nib = np.empty((g, p, n, 4), np.uint8)
        nib[..., 0::2] = words & 0xF
        nib[..., 1::2] = words >> 4
        vals = E2M1[nib]
    vals = vals * np.repeat(np.exp2(scales.astype(np.float64) - 127.0), 8, axis=1)[..., None]
    return vals.transpose(0, 1, 3, 2).reshape(g * 512, n)


def pack4(w):
    words, scales = pack_weight(w, "e2m1")
    return words.reshape(words.shape[0], 128, -1), scales


def unpack4(words, scales):
    return unpack_weight(words.reshape(words.shape[0], 128, -1, 2), scales, "e2m1")


B, S, I, O = 2, 256, 2048, 5632


def setup_inputs():
    s = mx_kscale(I)
    x = bf(np.random.standard_normal((B, S, I)) * s)
    W = np.random.standard_normal((I, O)) * 0.022 / s[:, None]
    w_words, w_scales = pack4(W)
    return {"input": x, "bias": bf(np.random.standard_normal(O) * 0.3), "w_words": w_words, "w_scales": w_scales}


def reference(input, bias, w_words, w_scales):
    w = unpack4(w_words, w_scales)
    return (mxq(f64(input), 2, "e4m3") @ w) + f64(bias)

@@ -1,0 +1,139 @@
+from contextlib import ExitStack
+
+import concourse.mybir as mybir
+from concourse.masks import make_identity
+
+F32 = mybir.dt.float32
+BF16 = mybir.dt.bfloat16
+I32 = mybir.dt.int32
+U32 = mybir.dt.uint32
+U8 = mybir.dt.uint8
+FP8X4 = mybir.dt.float8_e4m3fn_x4
+FP4X4 = mybir.dt.float4_e2m1fn_x4
+
+P = 128
+TOKENS = 512
+K = 2048
+N = 5632
+PASSES = K // 512
+M_TILES = TOKENS // P
+NT = 512
+N_TILES = N // NT
+
+FLOPS = 2 * TOKENS * K * N
+
+LOAD_GROUPS = [[0], [1, 2], [3, 4, 5, 6], [7, 8, 9, 10]]
+STORE_GROUPS = [[0], [1], [2, 3], [4, 5], [6, 7], [8, 9], [10]]
+
+
+def tile_mxlinear_kernel(tc, x, bias, w_words, w_scales, out):
+    nc = tc.nc
+    x_rows = x.flatten_outer_dims()
+    out_rows = out.flatten_outer_dims()
+    words_i32 = w_words.bitcast(I32)
+    scales_i32 = w_scales.bitcast(I32)
+
+    with ExitStack() as ctx:
+        keep = ctx.enter_context(tc.tile_pool(name="keep", bufs=1))
+        stage_pool = ctx.enter_context(tc.tile_pool(name="stage", bufs=20))
+        psum = ctx.enter_context(tc.psum_pool(name="psum", bufs=8))
+        ctx.enter_context(tc.manual_schedule())
+
+        ident = keep.tile([P, P], F32, name="ident")
+        make_identity(nc, ident[:])
+
+        bias_bc = keep.tile([P, N], BF16, name="bias_bc")
+        x_sb = [keep.tile([P, K], BF16, name="x_sb%d" % m) for m in range(M_TILES)]
+        grouped = [keep.tile([P, K], BF16, name="grouped%d" % m, align_bytes=64) for m in range(M_TILES)]
+        x_codes = keep.tile([P, M_TILES, PASSES * P], U32, name="x_codes", align_bytes=64)
+        x_planes = keep.tile([P, M_TILES, PASSES * P], U8, name="x_planes", align_bytes=64)
+        w_tiles = []
+        w_planes = []
+        where = {}
+        for i, grp in enumerate(LOAD_GROUPS):
+            cols = NT * len(grp)
+            w_tiles.append(keep.tile([P, PASSES, 2 * cols], U8, name="w_tile%d" % i, align_bytes=64))
+            w_planes.append(keep.tile([P, PASSES, cols], U8, name="w_plane%d" % i, align_bytes=64))
+            for j, n in enumerate(grp):
+                where[n] = (i, j)
+
+        for plane in w_planes:
+            nc.vector.memset(plane[:].bitcast(I32), 0)
+
+        for m in range(M_TILES):
+            nc.sync.dma_start(out=x_sb[m][:], in_=x_rows[P * m : P * (m + 1), :])
+        for i, grp in enumerate(LOAD_GROUPS):
+            c0 = NT * grp[0]
+            c1 = NT * (grp[-1] + 1)
+            nc.sync.dma_start(
+                out=w_tiles[i][:].bitcast(I32),
+                in_=words_i32[:, :, c0 // 2 : c1 // 2].rearrange("g p c -> p g c"),
+            )
+            for b in range(2):
+                for r in range(4):
+                    nc.sync.dma_start(
+                        out=w_planes[i][32 * b + r : P : 64, :, :].bitcast(I32),
+                        in_=scales_i32[:, 4 * b + r : 16 : 8, c0 // 4 : c1 // 4].rearrange("g h c -> h g c"),
+                    )
+            nc.sync.dma_start(out=bias_bc[:, c0:c1], in_=bias[c0:c1].partition_broadcast(P))
+
+        def transposes(m):
+            words = x_sb[m][:].bitcast(F32)
+            banks = []
+            for h in range(2):
+                xt = psum.tile([P, 2, 2, P], F32, tag="bank", name="xt")
+                for gl in range(2):
+                    g = 2 * h + gl
+                    for u in range(2):
+                        nc.tensor.transpose(xt[:, gl, u, :], words[:, 256 * g + u : 256 * (g + 1) : 2], ident[:])
+                banks.append(xt)
+            return banks
+
+        def copies(m, banks):
+            dst = grouped[m][:].bitcast(F32)
+            for h in range(2):
+                d = dst[:, 512 * h : 512 * (h + 1)].rearrange("p (g m u) -> p g m u", g=2, u=2)
+                s = banks[h][:].rearrange("p g u m -> p g m u")
+                if h == 0:
+                    nc.vector.tensor_copy(out=d, in_=s)
+                else:
+                    nc.scalar.copy(out=d, in_=s)
+
+        def quantise(m):
+            nc.vector.quantize_mx(
+                out=x_codes[:, m, :].bitcast(FP8X4),
+                scales=x_planes[:, m, :],
+                in_=grouped[m][:],
+            )
+
+        copies(0, transposes(0))
+        for m in range(1, M_TILES):
+            copies(m, transposes(m))
+            quantise(m - 1)
+        quantise(M_TILES - 1)
+
+        for grp in STORE_GROUPS:
+            c0 = NT * grp[0]
+            c1 = NT * (grp[-1] + 1)
+            for m in range(M_TILES):
+                stage = stage_pool.tile([P, 2 * NT], F32, tag="stage", name="stage")
+                for j, n in enumerate(grp):
+                    i, jj = where[n]
+                    acc = psum.tile([P, NT], F32, tag="bank", name="acc")
+                    for g in range(PASSES):
+                        nc.tensor.matmul_mx(
+                            out=acc[:],
+                            lhsT=x_codes[:, m, P * g : P * (g + 1)].bitcast(FP8X4),
+                            lhsT_scale=x_planes[:, m, P * g : P * (g + 1)],
+                            rhs=w_tiles[i][:, g, 2 * NT * jj : 2 * NT * (jj + 1)].bitcast(FP4X4),
+                            rhs_scale=w_planes[i][:, g, NT * jj : NT * (jj + 1)],
+                            start=(g == 0),
+                            stop=(g == PASSES - 1),
+                        )
+                    nc.vector.tensor_tensor(
+                        out=stage[:, NT * j : NT * (j + 1)],
+                        in0=acc[:],
+                        in1=bias_bc[:, NT * n : NT * (n + 1)],
+                        op=mybir.AluOpType.add,
+                    )
+                nc.sync.dma_start(out=out_rows[P * m : P * (m + 1), c0:c1], in_=stage[:, 0 : c1 - c0])

@@ -42,7 +42,10 @@ def tile_mxlinear_kernel(tc, x, bias, w_words, w_scales, out):
         ident = keep.tile([P, P], F32, name="ident")
         make_identity(nc, ident[:])
 
-        bias_bc = keep.tile([P, N], BF16, name="bias_bc")
+        ident_bf = keep.tile([P, P], BF16, name="ident_bf")
+        make_identity(nc, ident_bf[:])
+        bias_rows = keep.tile([P, NT], BF16, name="bias_rows")
+        bias_bc = keep.tile([P, N], F32, name="bias_bc")
         x_sb = [keep.tile([P, K], BF16, name="x_sb%d" % m) for m in range(M_TILES)]
         grouped = [keep.tile([P, K], BF16, name="grouped%d" % m, align_bytes=64) for m in range(M_TILES)]
         x_codes = keep.tile([P, M_TILES, PASSES * P], U32, name="x_codes", align_bytes=64)
@@ -57,6 +60,8 @@ def tile_mxlinear_kernel(tc, x, bias, w_words, w_scales, out):
             for j, n in enumerate(grp):
                 where[n] = (i, j)
 
+        nc.vector.memset(bias_rows[:].bitcast(I32), 0)
+        nc.scalar.dma_start(out=bias_rows[0:N_TILES, :], in_=bias.rearrange("(j n) -> j n", n=NT))
         for plane in w_planes:
             nc.vector.memset(plane[:].bitcast(I32), 0)
 
@@ -75,7 +80,6 @@ def tile_mxlinear_kernel(tc, x, bias, w_words, w_scales, out):
                         out=w_planes[i][32 * b + r : P : 64, :, :].bitcast(I32),
                         in_=scales_i32[:, 4 * b + r : 16 : 8, c0 // 4 : c1 // 4].rearrange("g h c -> h g c"),
                     )
-            nc.sync.dma_start(out=bias_bc[:, c0:c1], in_=bias[c0:c1].partition_broadcast(P))
 
         def transposes(m):
             words = x_sb[m][:].bitcast(F32)
@@ -106,15 +110,33 @@ def tile_mxlinear_kernel(tc, x, bias, w_words, w_scales, out):
                 in_=grouped[m][:],
             )
 
+        def spread_bias(n):
+            pb = psum.tile([P, NT], F32, tag="bank", name="pb")
+            nc.tensor.matmul(
+                out=pb[:],
+                lhsT=ident_bf[:, n : n + 1].to_broadcast([P, P]),
+                rhs=bias_rows[:],
+                start=True,
+                stop=True,
+            )
+            nc.scalar.copy(out=bias_bc[:, NT * n : NT * (n + 1)], in_=pb[:])
+
         copies(0, transposes(0))
         for m in range(1, M_TILES):
             copies(m, transposes(m))
             quantise(m - 1)
+        spread = 3
+        for n in range(spread):
+            spread_bias(n)
         quantise(M_TILES - 1)
 
-        for grp in STORE_GROUPS:
+        for ci, grp in enumerate(STORE_GROUPS):
             c0 = NT * grp[0]
             c1 = NT * (grp[-1] + 1)
+            ahead = STORE_GROUPS[min(ci + 1, len(STORE_GROUPS) - 1)][-1] + 1
+            for n in range(spread, ahead):
+                spread_bias(n)
+            spread = max(spread, ahead)
             for m in range(M_TILES):
                 stage = stage_pool.tile([P, 2 * NT], F32, tag="stage", name="stage")
                 for j, n in enumerate(grp):

@@ -22,8 +22,11 @@ N_TILES = N // NT
 
 FLOPS = 2 * TOKENS * K * N
 
-LOAD_GROUPS = [[0], [1, 2], [3, 4, 5, 6], [7, 8, 9, 10]]
+WORD_GROUPS = [[0], [1, 2], [3, 4, 5, 6], [7, 8, 9, 10]]
+SCALE_GROUPS = [[0, 1, 2], [3, 4, 5, 6], [7, 8, 9, 10]]
 STORE_GROUPS = [[0], [1], [2, 3], [4, 5], [6, 7], [8, 9], [10]]
+BIAS_AHEAD = [3, 3, 3, 2]
+TAPER = 128
 
 
 def tile_mxlinear_kernel(tc, x, bias, w_words, w_scales, out):
@@ -39,11 +42,11 @@ def tile_mxlinear_kernel(tc, x, bias, w_words, w_scales, out):
         psum = ctx.enter_context(tc.psum_pool(name="psum", bufs=8))
         ctx.enter_context(tc.manual_schedule())
 
+        ident_bf = keep.tile([P, P], BF16, name="ident_bf")
+        make_identity(nc, ident_bf[:])
         ident = keep.tile([P, P], F32, name="ident")
         make_identity(nc, ident[:])
 
-        ident_bf = keep.tile([P, P], BF16, name="ident_bf")
-        make_identity(nc, ident_bf[:])
         bias_rows = keep.tile([P, NT], BF16, name="bias_rows")
         bias_bc = keep.tile([P, N], F32, name="bias_bc")
         x_sb = [keep.tile([P, K], BF16, name="x_sb%d" % m) for m in range(M_TILES)]
@@ -51,35 +54,52 @@ def tile_mxlinear_kernel(tc, x, bias, w_words, w_scales, out):
         x_codes = keep.tile([P, M_TILES, PASSES * P], U32, name="x_codes", align_bytes=64)
         x_planes = keep.tile([P, M_TILES, PASSES * P], U8, name="x_planes", align_bytes=64)
         w_tiles = []
-        w_planes = []
-        where = {}
-        for i, grp in enumerate(LOAD_GROUPS):
-            cols = NT * len(grp)
-            w_tiles.append(keep.tile([P, PASSES, 2 * cols], U8, name="w_tile%d" % i, align_bytes=64))
-            w_planes.append(keep.tile([P, PASSES, cols], U8, name="w_plane%d" % i, align_bytes=64))
+        where_w = {}
+        for i, grp in enumerate(WORD_GROUPS):
+            w_tiles.append(keep.tile([P, PASSES, 2 * NT * len(grp)], U8, name="w_tile%d" % i, align_bytes=64))
             for j, n in enumerate(grp):
-                where[n] = (i, j)
+                where_w[n] = (i, j)
+        w_planes = []
+        where_s = {}
+        for i, grp in enumerate(SCALE_GROUPS):
+            w_planes.append(keep.tile([P, PASSES, NT * len(grp)], U8, name="w_plane%d" % i, align_bytes=64))
+            for j, n in enumerate(grp):
+                where_s[n] = (i, j)
 
         nc.vector.memset(bias_rows[:].bitcast(I32), 0)
         nc.scalar.dma_start(out=bias_rows[0:N_TILES, :], in_=bias.rearrange("(j n) -> j n", n=NT))
         for plane in w_planes:
             nc.vector.memset(plane[:].bitcast(I32), 0)
 
-        for m in range(M_TILES):
-            nc.sync.dma_start(out=x_sb[m][:], in_=x_rows[P * m : P * (m + 1), :])
-        for i, grp in enumerate(LOAD_GROUPS):
+        def load_words(i):
+            grp = WORD_GROUPS[i]
             c0 = NT * grp[0]
             c1 = NT * (grp[-1] + 1)
             nc.sync.dma_start(
                 out=w_tiles[i][:].bitcast(I32),
                 in_=words_i32[:, :, c0 // 2 : c1 // 2].rearrange("g p c -> p g c"),
             )
+
+        def load_scales(i):
+            grp = SCALE_GROUPS[i]
+            c0 = NT * grp[0]
+            c1 = NT * (grp[-1] + 1)
             for b in range(2):
                 for r in range(4):
                     nc.sync.dma_start(
                         out=w_planes[i][32 * b + r : P : 64, :, :].bitcast(I32),
                         in_=scales_i32[:, 4 * b + r : 16 : 8, c0 // 4 : c1 // 4].rearrange("g h c -> h g c"),
                     )
+
+        for m in range(M_TILES):
+            nc.sync.dma_start(out=x_sb[m][:], in_=x_rows[P * m : P * (m + 1), :])
+        load_scales(0)
+        load_words(0)
+        load_words(1)
+        load_scales(1)
+        load_words(2)
+        load_scales(2)
+        load_words(3)
 
         def transposes(m):
             words = x_sb[m][:].bitcast(F32)
@@ -98,10 +118,7 @@ def tile_mxlinear_kernel(tc, x, bias, w_words, w_scales, out):
             for h in range(2):
                 d = dst[:, 512 * h : 512 * (h + 1)].rearrange("p (g m u) -> p g m u", g=2, u=2)
                 s = banks[h][:].rearrange("p g u m -> p g m u")
-                if h == 0:
-                    nc.vector.tensor_copy(out=d, in_=s)
-                else:
-                    nc.scalar.copy(out=d, in_=s)
+                nc.vector.tensor_copy(out=d, in_=s)
 
         def quantise(m):
             nc.vector.quantize_mx(
@@ -121,41 +138,50 @@ def tile_mxlinear_kernel(tc, x, bias, w_words, w_scales, out):
             )
             nc.scalar.copy(out=bias_bc[:, NT * n : NT * (n + 1)], in_=pb[:])
 
-        copies(0, transposes(0))
-        for m in range(1, M_TILES):
+        spread = 0
+        for m in range(M_TILES):
+            for n in range(spread, spread + BIAS_AHEAD[m]):
+                spread_bias(n)
+            spread += BIAS_AHEAD[m]
             copies(m, transposes(m))
-            quantise(m - 1)
-        spread = 3
-        for n in range(spread):
-            spread_bias(n)
+            if m > 0:
+                quantise(m - 1)
         quantise(M_TILES - 1)
 
-        for ci, grp in enumerate(STORE_GROUPS):
+        def product(m, n, col, width, dest):
+            iw, jw = where_w[n]
+            js = where_s[n][1]
+            plane = w_planes[where_s[n][0]]
+            acc = psum.tile([P, width], F32, tag="bank", name="acc")
+            for g in range(PASSES):
+                nc.tensor.matmul_mx(
+                    out=acc[:],
+                    lhsT=x_codes[:, m, P * g : P * (g + 1)].bitcast(FP8X4),
+                    lhsT_scale=x_planes[:, m, P * g : P * (g + 1)],
+                    rhs=w_tiles[iw][:, g, 2 * (NT * jw + col) : 2 * (NT * jw + col + width)].bitcast(FP4X4),
+                    rhs_scale=plane[:, g, NT * js + col : NT * js + col + width],
+                    start=(g == 0),
+                    stop=(g == PASSES - 1),
+                )
+            nc.vector.tensor_tensor(
+                out=dest,
+                in0=acc[:],
+                in1=bias_bc[:, NT * n + col : NT * n + col + width],
+                op=mybir.AluOpType.add,
+            )
+
+        last = (M_TILES - 1, N_TILES - 1)
+        for grp in STORE_GROUPS:
             c0 = NT * grp[0]
             c1 = NT * (grp[-1] + 1)
-            ahead = STORE_GROUPS[min(ci + 1, len(STORE_GROUPS) - 1)][-1] + 1
-            for n in range(spread, ahead):
-                spread_bias(n)
-            spread = max(spread, ahead)
             for m in range(M_TILES):
+                rows = out_rows[P * m : P * (m + 1), :]
                 stage = stage_pool.tile([P, 2 * NT], F32, tag="stage", name="stage")
-                for j, n in enumerate(grp):
-                    i, jj = where[n]
-                    acc = psum.tile([P, NT], F32, tag="bank", name="acc")
-                    for g in range(PASSES):
-                        nc.tensor.matmul_mx(
-                            out=acc[:],
-                            lhsT=x_codes[:, m, P * g : P * (g + 1)].bitcast(FP8X4),
-                            lhsT_scale=x_planes[:, m, P * g : P * (g + 1)],
-                            rhs=w_tiles[i][:, g, 2 * NT * jj : 2 * NT * (jj + 1)].bitcast(FP4X4),
-                            rhs_scale=w_planes[i][:, g, NT * jj : NT * (jj + 1)],
-                            start=(g == 0),
-                            stop=(g == PASSES - 1),
-                        )
-                    nc.vector.tensor_tensor(
-                        out=stage[:, NT * j : NT * (j + 1)],
-                        in0=acc[:],
-                        in1=bias_bc[:, NT * n : NT * (n + 1)],
-                        op=mybir.AluOpType.add,
-                    )
-                nc.sync.dma_start(out=out_rows[P * m : P * (m + 1), c0:c1], in_=stage[:, 0 : c1 - c0])
+                if (m, grp[-1]) == last:
+                    for col in range(0, NT, TAPER):
+                        product(m, grp[0], col, TAPER, stage[:, col : col + TAPER])
+                        nc.sync.dma_start(out=rows[:, c0 + col : c0 + col + TAPER], in_=stage[:, col : col + TAPER])
+                else:
+                    for j, n in enumerate(grp):
+                        product(m, n, 0, NT, stage[:, NT * j : NT * (j + 1)])
+                    nc.sync.dma_start(out=rows[:, c0:c1], in_=stage[:, 0 : c1 - c0])

@@ -26,6 +26,7 @@ WORD_GROUPS = [[0], [1, 2], [3, 4, 5, 6], [7, 8, 9, 10]]
 SCALE_GROUPS = [[0, 1, 2], [3, 4, 5, 6], [7, 8, 9, 10]]
 STORE_GROUPS = [[0], [1], [2, 3], [4, 5], [6, 7], [8, 9], [10]]
 BIAS_AHEAD = [3, 3, 3, 2]
+QUANTISE_BEHIND = [[], [0], [1, 2], [3]]
 TAPER = 128
 
 
@@ -67,7 +68,7 @@ def tile_mxlinear_kernel(tc, x, bias, w_words, w_scales, out):
                 where_s[n] = (i, j)
 
         nc.vector.memset(bias_rows[:].bitcast(I32), 0)
-        nc.scalar.dma_start(out=bias_rows[0:N_TILES, :], in_=bias.rearrange("(j n) -> j n", n=NT))
+        nc.sync.dma_start(out=bias_rows[0:N_TILES, :], in_=bias.rearrange("(j n) -> j n", n=NT))
         for plane in w_planes:
             nc.vector.memset(plane[:].bitcast(I32), 0)
 
@@ -144,9 +145,8 @@ def tile_mxlinear_kernel(tc, x, bias, w_words, w_scales, out):
                 spread_bias(n)
             spread += BIAS_AHEAD[m]
             copies(m, transposes(m))
-            if m > 0:
-                quantise(m - 1)
-        quantise(M_TILES - 1)
+            for q in QUANTISE_BEHIND[m]:
+                quantise(q)
 
         def product(m, n, col, width, dest):
             iw, jw = where_w[n]

@@ -23,9 +23,11 @@ N_TILES = N // NT
 FLOPS = 2 * TOKENS * K * N
 
 WORD_GROUPS = [[0], [1, 2], [3, 4, 5, 6], [7, 8, 9, 10]]
-SCALE_GROUPS = [[0, 1, 2], [3, 4, 5, 6], [7, 8, 9, 10]]
+SCALE_GROUPS = [[0], [1, 2], [3, 4, 5, 6], [7, 8, 9, 10]]
 STORE_GROUPS = [[0], [1], [2, 3], [4, 5], [6, 7], [8, 9], [10]]
-BIAS_AHEAD = [3, 3, 3, 2]
+BIAS_PIECES = 16
+BIAS_COLS = N // BIAS_PIECES
+BIAS_AHEAD = [4, 4, 4, 4]
 QUANTISE_BEHIND = [[], [0], [1, 2], [3]]
 TAPER = 128
 
@@ -48,7 +50,7 @@ def tile_mxlinear_kernel(tc, x, bias, w_words, w_scales, out):
         ident = keep.tile([P, P], F32, name="ident")
         make_identity(nc, ident[:])
 
-        bias_rows = keep.tile([P, NT], BF16, name="bias_rows")
+        bias_rows = keep.tile([P, BIAS_COLS], BF16, name="bias_rows")
         bias_bc = keep.tile([P, N], F32, name="bias_bc")
         x_sb = [keep.tile([P, K], BF16, name="x_sb%d" % m) for m in range(M_TILES)]
         grouped = [keep.tile([P, K], BF16, name="grouped%d" % m, align_bytes=64) for m in range(M_TILES)]
@@ -67,8 +69,12 @@ def tile_mxlinear_kernel(tc, x, bias, w_words, w_scales, out):
             for j, n in enumerate(grp):
                 where_s[n] = (i, j)
 
-        nc.vector.memset(bias_rows[:].bitcast(I32), 0)
-        nc.sync.dma_start(out=bias_rows[0:N_TILES, :], in_=bias.rearrange("(j n) -> j n", n=NT))
+        nc.sync.dma_start(
+            out=bias_rows[:],
+            in_=bias.rearrange("(j n) -> j n", n=BIAS_COLS)
+            .unsqueeze(0)
+            .to_broadcast([P // BIAS_PIECES, BIAS_PIECES, BIAS_COLS]),
+        )
         for plane in w_planes:
             nc.vector.memset(plane[:].bitcast(I32), 0)
 
@@ -85,22 +91,18 @@ def tile_mxlinear_kernel(tc, x, bias, w_words, w_scales, out):
             grp = SCALE_GROUPS[i]
             c0 = NT * grp[0]
             c1 = NT * (grp[-1] + 1)
-            for b in range(2):
-                for r in range(4):
-                    nc.sync.dma_start(
-                        out=w_planes[i][32 * b + r : P : 64, :, :].bitcast(I32),
-                        in_=scales_i32[:, 4 * b + r : 16 : 8, c0 // 4 : c1 // 4].rearrange("g h c -> h g c"),
-                    )
+            step = 4 if i == 0 else 8
+            for q in range(step):
+                nc.sync.dma_start(
+                    out=w_planes[i][32 * (q // 4) + q % 4 : P : 8 * step, :, :].bitcast(I32),
+                    in_=scales_i32[:, q:16:step, c0 // 4 : c1 // 4].rearrange("g h c -> h g c"),
+                )
 
         for m in range(M_TILES):
             nc.sync.dma_start(out=x_sb[m][:], in_=x_rows[P * m : P * (m + 1), :])
-        load_scales(0)
-        load_words(0)
-        load_words(1)
-        load_scales(1)
-        load_words(2)
-        load_scales(2)
-        load_words(3)
+        for i in range(len(WORD_GROUPS)):
+            load_words(i)
+            load_scales(i)
 
         def transposes(m):
             words = x_sb[m][:].bitcast(F32)
@@ -128,16 +130,16 @@ def tile_mxlinear_kernel(tc, x, bias, w_words, w_scales, out):
                 in_=grouped[m][:],
             )
 
-        def spread_bias(n):
-            pb = psum.tile([P, NT], F32, tag="bank", name="pb")
+        def spread_bias(j):
+            pb = psum.tile([P, BIAS_COLS], F32, tag="bank", name="pb")
             nc.tensor.matmul(
                 out=pb[:],
-                lhsT=ident_bf[:, n : n + 1].to_broadcast([P, P]),
+                lhsT=ident_bf[:, j : j + 1].to_broadcast([P, P]),
                 rhs=bias_rows[:],
                 start=True,
                 stop=True,
             )
-            nc.scalar.copy(out=bias_bc[:, NT * n : NT * (n + 1)], in_=pb[:])
+            nc.scalar.copy(out=bias_bc[:, BIAS_COLS * j : BIAS_COLS * (j + 1)], in_=pb[:])
 
         spread = 0
         for m in range(M_TILES):

@@ -25,11 +25,11 @@ FLOPS = 2 * TOKENS * K * N
 WORD_GROUPS = [[0], [1, 2], [3, 4, 5, 6], [7, 8, 9, 10]]
 SCALE_GROUPS = [[0], [1, 2], [3, 4, 5, 6], [7, 8, 9, 10]]
 STORE_GROUPS = [[0], [1], [2, 3], [4, 5], [6, 7], [8, 9], [10]]
-BIAS_PIECES = 16
-BIAS_COLS = N // BIAS_PIECES
-BIAS_AHEAD = [4, 4, 4, 4]
-QUANTISE_BEHIND = [[], [0], [1, 2], [3]]
 TAPER = 128
+
+Q = 32
+BIAS_BLOCK_BASE = [0, 32, 56]
+BIAS_PIECES = [(0, 0, 8), (0, 8, 24), (1, 0, 32), (2, 8, 24)]
 
 
 def tile_mxlinear_kernel(tc, x, bias, w_words, w_scales, out):
@@ -45,13 +45,16 @@ def tile_mxlinear_kernel(tc, x, bias, w_words, w_scales, out):
         psum = ctx.enter_context(tc.psum_pool(name="psum", bufs=8))
         ctx.enter_context(tc.manual_schedule())
 
-        ident_bf = keep.tile([P, P], BF16, name="ident_bf")
-        make_identity(nc, ident_bf[:])
         ident = keep.tile([P, P], F32, name="ident")
         make_identity(nc, ident[:])
 
-        bias_rows = keep.tile([P, BIAS_COLS], BF16, name="bias_rows")
-        bias_bc = keep.tile([P, N], F32, name="bias_bc")
+        bias_l = keep.tile([P, len(BIAS_BLOCK_BASE), 2 * Q], BF16, name="bias_l", align_bytes=64)
+        bias_lt = keep.tile([P, len(BIAS_BLOCK_BASE), Q], F32, name="bias_lt", align_bytes=64)
+        bias_wide = [
+            keep.tile([P, rows * Q], F32, name="bias_wide%d" % i, align_bytes=64)
+            for i, (blk, first, rows) in enumerate(BIAS_PIECES)
+        ]
+        bias_bc = keep.tile([P, N], BF16, name="bias_bc", align_bytes=64)
         x_sb = [keep.tile([P, K], BF16, name="x_sb%d" % m) for m in range(M_TILES)]
         grouped = [keep.tile([P, K], BF16, name="grouped%d" % m, align_bytes=64) for m in range(M_TILES)]
         x_codes = keep.tile([P, M_TILES, PASSES * P], U32, name="x_codes", align_bytes=64)
@@ -69,12 +72,15 @@ def tile_mxlinear_kernel(tc, x, bias, w_words, w_scales, out):
             for j, n in enumerate(grp):
                 where_s[n] = (i, j)
 
-        nc.sync.dma_start(
-            out=bias_rows[:],
-            in_=bias.rearrange("(j n) -> j n", n=BIAS_COLS)
-            .unsqueeze(0)
-            .to_broadcast([P // BIAS_PIECES, BIAS_PIECES, BIAS_COLS]),
-        )
+        for blk, base in enumerate(BIAS_BLOCK_BASE):
+            nc.scalar.dma_start(
+                out=bias_l[:, blk, :],
+                in_=bias[2 * Q * base : 2 * Q * (base + Q)]
+                .rearrange("(r j) -> r j", j=2 * Q)
+                .unsqueeze(0)
+                .to_broadcast([P // Q, Q, 2 * Q]),
+            )
+
         for plane in w_planes:
             nc.vector.memset(plane[:].bitcast(I32), 0)
 
@@ -82,10 +88,14 @@ def tile_mxlinear_kernel(tc, x, bias, w_words, w_scales, out):
             grp = WORD_GROUPS[i]
             c0 = NT * grp[0]
             c1 = NT * (grp[-1] + 1)
-            nc.sync.dma_start(
-                out=w_tiles[i][:].bitcast(I32),
-                in_=words_i32[:, :, c0 // 2 : c1 // 2].rearrange("g p c -> p g c"),
-            )
+            if i == 0:
+                for g in range(PASSES):
+                    nc.sync.dma_start(out=w_tiles[i][:, g, :].bitcast(I32), in_=words_i32[g, :, c0 // 2 : c1 // 2])
+            else:
+                nc.sync.dma_start(
+                    out=w_tiles[i][:].bitcast(I32),
+                    in_=words_i32[:, :, c0 // 2 : c1 // 2].rearrange("g p c -> p g c"),
+                )
 
         def load_scales(i):
             grp = SCALE_GROUPS[i]
@@ -100,7 +110,9 @@ def tile_mxlinear_kernel(tc, x, bias, w_words, w_scales, out):
 
         for m in range(M_TILES):
             nc.sync.dma_start(out=x_sb[m][:], in_=x_rows[P * m : P * (m + 1), :])
-        for i in range(len(WORD_GROUPS)):
+        load_scales(0)
+        load_words(0)
+        for i in range(1, len(WORD_GROUPS)):
             load_words(i)
             load_scales(i)
 
@@ -121,7 +133,10 @@ def tile_mxlinear_kernel(tc, x, bias, w_words, w_scales, out):
             for h in range(2):
                 d = dst[:, 512 * h : 512 * (h + 1)].rearrange("p (g m u) -> p g m u", g=2, u=2)
                 s = banks[h][:].rearrange("p g u m -> p g m u")
-                nc.vector.tensor_copy(out=d, in_=s)
+                if h == 0:
+                    nc.vector.tensor_copy(out=d, in_=s)
+                else:
+                    nc.scalar.copy(out=d, in_=s)
 
         def quantise(m):
             nc.vector.quantize_mx(
@@ -130,25 +145,36 @@ def tile_mxlinear_kernel(tc, x, bias, w_words, w_scales, out):
                 in_=grouped[m][:],
             )
 
-        def spread_bias(j):
-            pb = psum.tile([P, BIAS_COLS], F32, tag="bank", name="pb")
-            nc.tensor.matmul(
-                out=pb[:],
-                lhsT=ident_bf[:, j : j + 1].to_broadcast([P, P]),
-                rhs=bias_rows[:],
-                start=True,
-                stop=True,
-            )
-            nc.scalar.copy(out=bias_bc[:, BIAS_COLS * j : BIAS_COLS * (j + 1)], in_=pb[:])
+        def bias_turn():
+            for blk in range(len(BIAS_BLOCK_BASE)):
+                nc.vector.transpose(out=bias_lt[:, blk, :], in_=bias_l[:, blk, :].bitcast(F32))
 
-        spread = 0
-        for m in range(M_TILES):
-            for n in range(spread, spread + BIAS_AHEAD[m]):
-                spread_bias(n)
-            spread += BIAS_AHEAD[m]
-            copies(m, transposes(m))
-            for q in QUANTISE_BEHIND[m]:
-                quantise(q)
+        def bias_widen(i):
+            blk, first, rows = BIAS_PIECES[i]
+            nc.scalar.copy(
+                out=bias_wide[i][:].rearrange("p (r i) -> p r i", i=Q),
+                in_=bias_lt[:, blk, first : first + rows].unsqueeze(2).to_broadcast([P, rows, Q]),
+            )
+
+        def bias_spread(i):
+            blk, first, rows = BIAS_PIECES[i]
+            row0 = BIAS_BLOCK_BASE[blk] + first
+            nc.vector.transpose(out=bias_bc[:].bitcast(F32)[:, Q * row0 : Q * (row0 + rows)], in_=bias_wide[i][:])
+
+        copies(0, transposes(0))
+        copies(1, transposes(1))
+        quantise(0)
+        bias_turn()
+        bias_widen(0)
+        copies(2, transposes(2))
+        quantise(1)
+        copies(3, transposes(3))
+        bias_spread(0)
+        quantise(2)
+        quantise(3)
+        for i in range(1, len(BIAS_PIECES)):
+            bias_widen(i)
+        bias_spread(1)
 
         def product(m, n, col, width, dest):
             iw, jw = where_w[n]
@@ -173,7 +199,7 @@ def tile_mxlinear_kernel(tc, x, bias, w_words, w_scales, out):
             )
 
         last = (M_TILES - 1, N_TILES - 1)
-        for grp in STORE_GROUPS:
+        for ci, grp in enumerate(STORE_GROUPS):
             c0 = NT * grp[0]
             c1 = NT * (grp[-1] + 1)
             for m in range(M_TILES):
@@ -187,3 +213,5 @@ def tile_mxlinear_kernel(tc, x, bias, w_words, w_scales, out):
                     for j, n in enumerate(grp):
                         product(m, n, 0, NT, stage[:, NT * j : NT * (j + 1)])
                     nc.sync.dma_start(out=rows[:, c0:c1], in_=stage[:, 0 : c1 - c0])
+            if ci + 2 < len(BIAS_PIECES):
+                bias_spread(ci + 2)

@@ -72,8 +72,9 @@ def tile_mxlinear_kernel(tc, x, bias, w_words, w_scales, out):
             for j, n in enumerate(grp):
                 where_s[n] = (i, j)
 
-        for blk, base in enumerate(BIAS_BLOCK_BASE):
-            nc.scalar.dma_start(
+        def load_bias(blk):
+            base = BIAS_BLOCK_BASE[blk]
+            nc.sync.dma_start(
                 out=bias_l[:, blk, :],
                 in_=bias[2 * Q * base : 2 * Q * (base + Q)]
                 .rearrange("(r j) -> r j", j=2 * Q)
@@ -108,11 +109,16 @@ def tile_mxlinear_kernel(tc, x, bias, w_words, w_scales, out):
                     in_=scales_i32[:, q:16:step, c0 // 4 : c1 // 4].rearrange("g h c -> h g c"),
                 )
 
+        load_bias(0)
         for m in range(M_TILES):
             nc.sync.dma_start(out=x_sb[m][:], in_=x_rows[P * m : P * (m + 1), :])
         load_scales(0)
         load_words(0)
-        for i in range(1, len(WORD_GROUPS)):
+        load_words(1)
+        load_bias(1)
+        load_bias(2)
+        load_scales(1)
+        for i in range(2, len(WORD_GROUPS)):
             load_words(i)
             load_scales(i)
 
@@ -145,9 +151,8 @@ def tile_mxlinear_kernel(tc, x, bias, w_words, w_scales, out):
                 in_=grouped[m][:],
             )
 
-        def bias_turn():
-            for blk in range(len(BIAS_BLOCK_BASE)):
-                nc.vector.transpose(out=bias_lt[:, blk, :], in_=bias_l[:, blk, :].bitcast(F32))
+        def bias_turn(blk):
+            nc.vector.transpose(out=bias_lt[:, blk, :], in_=bias_l[:, blk, :].bitcast(F32))
 
         def bias_widen(i):
             blk, first, rows = BIAS_PIECES[i]
@@ -164,17 +169,15 @@ def tile_mxlinear_kernel(tc, x, bias, w_words, w_scales, out):
         copies(0, transposes(0))
         copies(1, transposes(1))
         quantise(0)
-        bias_turn()
-        bias_widen(0)
         copies(2, transposes(2))
         quantise(1)
         copies(3, transposes(3))
-        bias_spread(0)
         quantise(2)
+        bias_turn(0)
+        bias_widen(0)
+        bias_widen(1)
         quantise(3)
-        for i in range(1, len(BIAS_PIECES)):
-            bias_widen(i)
-        bias_spread(1)
+        bias_spread(0)
 
         def product(m, n, col, width, dest):
             iw, jw = where_w[n]
@@ -213,5 +216,11 @@ def tile_mxlinear_kernel(tc, x, bias, w_words, w_scales, out):
                     for j, n in enumerate(grp):
                         product(m, n, 0, NT, stage[:, NT * j : NT * (j + 1)])
                     nc.sync.dma_start(out=rows[:, c0:c1], in_=stage[:, 0 : c1 - c0])
-            if ci + 2 < len(BIAS_PIECES):
-                bias_spread(ci + 2)
+            if ci == 0:
+                bias_spread(1)
+                bias_turn(1)
+                bias_turn(2)
+                bias_widen(2)
+                bias_widen(3)
+            elif ci + 1 < len(BIAS_PIECES):
+                bias_spread(ci + 1)

@@ -22,8 +22,8 @@ N_TILES = N // NT
 
 FLOPS = 2 * TOKENS * K * N
 
-WORD_GROUPS = [[0], [1, 2], [3, 4, 5, 6], [7, 8, 9, 10]]
-SCALE_GROUPS = [[0], [1, 2], [3, 4, 5, 6], [7, 8, 9, 10]]
+WORD_GROUPS = [[0], [1], [2], [3, 4], [5, 6], [7, 8], [9, 10]]
+SCALE_GROUPS = [[0, 1], [2, 3, 4], [5, 6, 7, 8, 9, 10]]
 STORE_GROUPS = [[0], [1], [2, 3], [4, 5], [6, 7], [8, 9], [10]]
 TAPER = 128
 
@@ -102,25 +102,32 @@ def tile_mxlinear_kernel(tc, x, bias, w_words, w_scales, out):
             grp = SCALE_GROUPS[i]
             c0 = NT * grp[0]
             c1 = NT * (grp[-1] + 1)
-            step = 4 if i == 0 else 8
-            for q in range(step):
+            for r in range(4):
                 nc.sync.dma_start(
-                    out=w_planes[i][32 * (q // 4) + q % 4 : P : 8 * step, :, :].bitcast(I32),
-                    in_=scales_i32[:, q:16:step, c0 // 4 : c1 // 4].rearrange("g h c -> h g c"),
+                    out=w_planes[i][r:P:32, :, :].bitcast(I32),
+                    in_=scales_i32[:, r:16:4, c0 // 4 : c1 // 4].rearrange("g h c -> h g c"),
                 )
 
-        load_bias(0)
-        for m in range(M_TILES):
+        def load_x(m):
             nc.sync.dma_start(out=x_sb[m][:], in_=x_rows[P * m : P * (m + 1), :])
+
+        load_x(0)
         load_scales(0)
+        load_x(1)
+        load_x(2)
+        load_x(3)
+        load_bias(0)
         load_words(0)
         load_words(1)
+        load_scales(1)
+        load_words(2)
         load_bias(1)
         load_bias(2)
-        load_scales(1)
-        for i in range(2, len(WORD_GROUPS)):
-            load_words(i)
-            load_scales(i)
+        load_words(3)
+        load_scales(2)
+        load_words(4)
+        load_words(5)
+        load_words(6)
 
         def transposes(m):
             words = x_sb[m][:].bitcast(F32)
@@ -173,10 +180,10 @@ def tile_mxlinear_kernel(tc, x, bias, w_words, w_scales, out):
         quantise(1)
         copies(3, transposes(3))
         quantise(2)
+        quantise(3)
         bias_turn(0)
         bias_widen(0)
         bias_widen(1)
-        quantise(3)
         bias_spread(0)
 
         def product(m, n, col, width, dest):
@@ -216,11 +223,13 @@ def tile_mxlinear_kernel(tc, x, bias, w_words, w_scales, out):
                     for j, n in enumerate(grp):
                         product(m, n, 0, NT, stage[:, NT * j : NT * (j + 1)])
                     nc.sync.dma_start(out=rows[:, c0:c1], in_=stage[:, 0 : c1 - c0])
-            if ci == 0:
-                bias_spread(1)
-                bias_turn(1)
-                bias_turn(2)
-                bias_widen(2)
-                bias_widen(3)
-            elif ci + 1 < len(BIAS_PIECES):
-                bias_spread(ci + 1)
+                if (ci, m) == (0, M_TILES - 1):
+                    bias_spread(1)
+                elif (ci, m) == (2, 1):
+                    bias_turn(1)
+                    bias_turn(2)
+                    bias_widen(2)
+                    bias_widen(3)
+                elif (ci, m) == (2, M_TILES - 1):
+                    bias_spread(2)
+                    bias_spread(3)

from contextlib import ExitStack

import concourse.mybir as mybir
from concourse.masks import make_identity

F32 = mybir.dt.float32
BF16 = mybir.dt.bfloat16
I32 = mybir.dt.int32
U32 = mybir.dt.uint32
U8 = mybir.dt.uint8
FP8X4 = mybir.dt.float8_e4m3fn_x4
FP4X4 = mybir.dt.float4_e2m1fn_x4

P = 128
TOKENS = 512
K = 2048
N = 5632
PASSES = K // 512
M_TILES = TOKENS // P
NT = 512
N_TILES = N // NT

FLOPS = 2 * TOKENS * K * N

WORD_GROUPS = [[0], [1], [2], [3, 4], [5, 6], [7, 8], [9, 10]]
SCALE_GROUPS = [[0, 1], [2, 3, 4], [5, 6, 7, 8, 9, 10]]
STORE_GROUPS = [[0], [1], [2, 3], [4, 5], [6, 7], [8, 9], [10]]
TAPER = 128

Q = 32
BIAS_BLOCK_BASE = [0, 32, 56]
BIAS_PIECES = [(0, 0, 8), (0, 8, 24), (1, 0, 32), (2, 8, 24)]


def tile_mxlinear_kernel(tc, x, bias, w_words, w_scales, out):
    nc = tc.nc
    x_rows = x.flatten_outer_dims()
    out_rows = out.flatten_outer_dims()
    words_i32 = w_words.bitcast(I32)
    scales_i32 = w_scales.bitcast(I32)

    with ExitStack() as ctx:
        keep = ctx.enter_context(tc.tile_pool(name="keep", bufs=1))
        stage_pool = ctx.enter_context(tc.tile_pool(name="stage", bufs=20))
        psum = ctx.enter_context(tc.psum_pool(name="psum", bufs=8))
        ctx.enter_context(tc.manual_schedule())

        ident = keep.tile([P, P], F32, name="ident")
        make_identity(nc, ident[:])

        bias_l = keep.tile([P, len(BIAS_BLOCK_BASE), 2 * Q], BF16, name="bias_l", align_bytes=64)
        bias_lt = keep.tile([P, len(BIAS_BLOCK_BASE), Q], F32, name="bias_lt", align_bytes=64)
        bias_wide = [
            keep.tile([P, rows * Q], F32, name="bias_wide%d" % i, align_bytes=64)
            for i, (blk, first, rows) in enumerate(BIAS_PIECES)
        ]
        bias_bc = keep.tile([P, N], BF16, name="bias_bc", align_bytes=64)
        x_sb = [keep.tile([P, K], BF16, name="x_sb%d" % m) for m in range(M_TILES)]
        grouped = [keep.tile([P, K], BF16, name="grouped%d" % m, align_bytes=64) for m in range(M_TILES)]
        x_codes = keep.tile([P, M_TILES, PASSES * P], U32, name="x_codes", align_bytes=64)
        x_planes = keep.tile([P, M_TILES, PASSES * P], U8, name="x_planes", align_bytes=64)
        w_tiles = []
        where_w = {}
        for i, grp in enumerate(WORD_GROUPS):
            w_tiles.append(keep.tile([P, PASSES, 2 * NT * len(grp)], U8, name="w_tile%d" % i, align_bytes=64))
            for j, n in enumerate(grp):
                where_w[n] = (i, j)
        w_planes = []
        where_s = {}
        for i, grp in enumerate(SCALE_GROUPS):
            w_planes.append(keep.tile([P, PASSES, NT * len(grp)], U8, name="w_plane%d" % i, align_bytes=64))
            for j, n in enumerate(grp):
                where_s[n] = (i, j)

        def load_bias(blk):
            base = BIAS_BLOCK_BASE[blk]
            nc.sync.dma_start(
                out=bias_l[:, blk, :],
                in_=bias[2 * Q * base : 2 * Q * (base + Q)]
                .rearrange("(r j) -> r j", j=2 * Q)
                .unsqueeze(0)
                .to_broadcast([P // Q, Q, 2 * Q]),
            )

        for plane in w_planes:
            nc.vector.memset(plane[:].bitcast(I32), 0)

        def load_words(i):
            grp = WORD_GROUPS[i]
            c0 = NT * grp[0]
            c1 = NT * (grp[-1] + 1)
            if i == 0:
                for g in range(PASSES):
                    nc.sync.dma_start(out=w_tiles[i][:, g, :].bitcast(I32), in_=words_i32[g, :, c0 // 2 : c1 // 2])
            else:
                nc.sync.dma_start(
                    out=w_tiles[i][:].bitcast(I32),
                    in_=words_i32[:, :, c0 // 2 : c1 // 2].rearrange("g p c -> p g c"),
                )

        def load_scales(i):
            grp = SCALE_GROUPS[i]
            c0 = NT * grp[0]
            c1 = NT * (grp[-1] + 1)
            for r in range(4):
                nc.sync.dma_start(
                    out=w_planes[i][r:P:32, :, :].bitcast(I32),
                    in_=scales_i32[:, r:16:4, c0 // 4 : c1 // 4].rearrange("g h c -> h g c"),
                )

        def load_x(m):
            nc.sync.dma_start(out=x_sb[m][:], in_=x_rows[P * m : P * (m + 1), :])

        load_x(0)
        load_scales(0)
        load_x(1)
        load_x(2)
        load_x(3)
        load_bias(0)
        load_words(0)
        load_words(1)
        load_scales(1)
        load_words(2)
        load_bias(1)
        load_bias(2)
        load_words(3)
        load_scales(2)
        load_words(4)
        load_words(5)
        load_words(6)

        def transposes(m):
            words = x_sb[m][:].bitcast(F32)
            banks = []
            for h in range(2):
                xt = psum.tile([P, 2, 2, P], F32, tag="bank", name="xt")
                for gl in range(2):
                    g = 2 * h + gl
                    for u in range(2):
                        nc.tensor.transpose(xt[:, gl, u, :], words[:, 256 * g + u : 256 * (g + 1) : 2], ident[:])
                banks.append(xt)
            return banks

        def copies(m, banks):
            dst = grouped[m][:].bitcast(F32)
            for h in range(2):
                d = dst[:, 512 * h : 512 * (h + 1)].rearrange("p (g m u) -> p g m u", g=2, u=2)
                s = banks[h][:].rearrange("p g u m -> p g m u")
                if h == 0:
                    nc.vector.tensor_copy(out=d, in_=s)
                else:
                    nc.scalar.copy(out=d, in_=s)

        def quantise(m):
            nc.vector.quantize_mx(
                out=x_codes[:, m, :].bitcast(FP8X4),
                scales=x_planes[:, m, :],
                in_=grouped[m][:],
            )

        def bias_turn(blk):
            nc.vector.transpose(out=bias_lt[:, blk, :], in_=bias_l[:, blk, :].bitcast(F32))

        def bias_widen(i):
            blk, first, rows = BIAS_PIECES[i]
            nc.scalar.copy(
                out=bias_wide[i][:].rearrange("p (r i) -> p r i", i=Q),
                in_=bias_lt[:, blk, first : first + rows].unsqueeze(2).to_broadcast([P, rows, Q]),
            )

        def bias_spread(i):
            blk, first, rows = BIAS_PIECES[i]
            row0 = BIAS_BLOCK_BASE[blk] + first
            nc.vector.transpose(out=bias_bc[:].bitcast(F32)[:, Q * row0 : Q * (row0 + rows)], in_=bias_wide[i][:])

        copies(0, transposes(0))
        copies(1, transposes(1))
        quantise(0)
        copies(2, transposes(2))
        quantise(1)
        copies(3, transposes(3))
        quantise(2)
        quantise(3)
        bias_turn(0)
        bias_widen(0)
        bias_widen(1)
        bias_spread(0)

        def product(m, n, col, width, dest):
            iw, jw = where_w[n]
            js = where_s[n][1]
            plane = w_planes[where_s[n][0]]
            acc = psum.tile([P, width], F32, tag="bank", name="acc")
            for g in range(PASSES):
                nc.tensor.matmul_mx(
                    out=acc[:],
                    lhsT=x_codes[:, m, P * g : P * (g + 1)].bitcast(FP8X4),
                    lhsT_scale=x_planes[:, m, P * g : P * (g + 1)],
                    rhs=w_tiles[iw][:, g, 2 * (NT * jw + col) : 2 * (NT * jw + col + width)].bitcast(FP4X4),
                    rhs_scale=plane[:, g, NT * js + col : NT * js + col + width],
                    start=(g == 0),
                    stop=(g == PASSES - 1),
                )
            nc.vector.tensor_tensor(
                out=dest,
                in0=acc[:],
                in1=bias_bc[:, NT * n + col : NT * n + col + width],
                op=mybir.AluOpType.add,
            )

        last = (M_TILES - 1, N_TILES - 1)
        for ci, grp in enumerate(STORE_GROUPS):
            c0 = NT * grp[0]
            c1 = NT * (grp[-1] + 1)
            for m in range(M_TILES):
                rows = out_rows[P * m : P * (m + 1), :]
                stage = stage_pool.tile([P, 2 * NT], F32, tag="stage", name="stage")
                if (m, grp[-1]) == last:
                    for col in range(0, NT, TAPER):
                        product(m, grp[0], col, TAPER, stage[:, col : col + TAPER])
                        nc.sync.dma_start(out=rows[:, c0 + col : c0 + col + TAPER], in_=stage[:, col : col + TAPER])
                else:
                    for j, n in enumerate(grp):
                        product(m, n, 0, NT, stage[:, NT * j : NT * (j + 1)])
                    nc.sync.dma_start(out=rows[:, c0:c1], in_=stage[:, 0 : c1 - c0])
                if (ci, m) == (0, M_TILES - 1):
                    bias_spread(1)
                elif (ci, m) == (2, 1):
                    bias_turn(1)
                    bias_turn(2)
                    bias_widen(2)
                    bias_widen(3)
                elif (ci, m) == (2, M_TILES - 1):
                    bias_spread(2)
                    bias_spread(3)
